import numpy as np
import ml_dtypes


def mxq(x, axis, fmt="e4m3"):
    dtype, down = {"e4m3": (ml_dtypes.float8_e4m3fn, 7), "e5m2": (ml_dtypes.float8_e5m2, 14)}[fmt]
    v = np.moveaxis(np.asarray(x, np.float32).astype(ml_dtypes.bfloat16).astype(np.float64), axis, -1)
    blocks = v.reshape(v.shape[:-1] + (-1, 32))
    amax = np.abs(blocks).max(-1, keepdims=True)
    byte = np.maximum(np.where(amax > 0, np.frexp(amax)[1] - 1 + 127, 0) - down, 1)
    scale = np.exp2(byte - 127.0)
    codes = (blocks / scale).astype(np.float32).astype(dtype).astype(np.float64)
    return np.moveaxis((codes * scale).reshape(v.shape), -1, axis)


WIDE = False


def mx_kscale(k):
    if not WIDE:
        return np.ones(k)
    levels = np.array([10, -10, 5, -5, 0])
    a = np.random.permutation(np.resize(levels, k // 512 * 4)).reshape(k // 512, 4)
    idx = np.arange(k)
    return np.exp2(a[idx // 512, idx % 128 // 32])


BF16 = ml_dtypes.bfloat16


def bf(x):
    return np.asarray(x, np.float32).astype(BF16)


def f64(x):
    return np.asarray(x).astype(np.float64)


E2M1 = np.array([0.0, 0.5, 1.0, 1.5, 2.0, 3.0, 4.0, 6.0, -0.0, -0.5, -1.0, -1.5, -2.0, -3.0, -4.0, -6.0])


def pack_weight(w, fmt):
    k, n = w.shape
    w = f64(bf(w)).reshape(k // 32, 32, n)
    amax = np.abs(w).max(1)
    if fmt == "e4m3":
        byte = np.frexp(amax)[1] - 1 + 127 - 7
    else:
        mant, ex = np.frexp(amax / 6.0)
        byte = np.where(mant > 0.5, ex, ex - 1) + 127
    byte = np.clip(np.where(amax > 0, byte, 1), 1, 254)
    scaled = (w * np.exp2(127.0 - byte)[:, None, :]).reshape(k, n).astype(np.float32)
    by_word = np.ascontiguousarray(scaled.reshape(k // 512, 128, 4, n).transpose(0, 1, 3, 2))
    if fmt == "e4m3":
        words = by_word.astype(ml_dtypes.float8_e4m3fn).view(np.uint8)
    else:
        c = by_word.astype(ml_dtypes.float4_e2m1fn).view(np.uint8) & 0xF
        words = c[..., 0::2] | (c[..., 1::2] << 4)
    return np.ascontiguousarray(words), np.ascontiguousarray(byte.astype(np.uint8).reshape(k // 512, 16, n))


def unpack_weight(words, scales, fmt):
    g, p, n, _ = words.shape
    if fmt == "e4m3":
        vals = np.ascontiguousarray(words).view(ml_dtypes.float8_e4m3fn).astype(np.float64)
    else:
        nib = np.empty((g, p, n, 4), np.uint8)
        nib[..., 0::2] = words & 0xF
        nib[..., 1::2] = words >> 4
        vals = E2M1[nib]
    vals = vals * np.repeat(np.exp2(scales.astype(np.float64) - 127.0), 8, axis=1)[..., None]
    return vals.transpose(0, 1, 3, 2).reshape(g * 512, n)


S, M, L1, L2, L3, B, NG = 512, 512, 1024, 8192, 512, 256, 4
FMT = "e4m3"


def sigmoid(v):
    return 1.0 / (1.0 + np.exp(-v))


def lstm_cell(x, h, c, Wih_t, Whh_t, bih, bhh):
    g = (mxq(x, 1, "e4m3") @ Wih_t) + (mxq(h, 1, "e4m3") @ Whh_t) + (bih + bhh)
    i, f, gg, o = np.split(g, NG, axis=-1)
    c_new = sigmoid(f) * c + sigmoid(i) * np.tanh(gg)
    h_new = sigmoid(o) * np.tanh(c_new)
    return h_new, c_new


def log_softmax(v):
    shifted = v - v.max(-1, keepdims=True)
    return shifted - np.log(np.exp(shifted).sum(-1, keepdims=True))


def setup_inputs():
    rn = np.random.standard_normal
    s, t2, t3 = mx_kscale(S), mx_kscale(L2), mx_kscale(L3)
    x = bf(rn((B, S)) * s)
    y2 = bf(rn((B, L2)) * 0.3 * t2)
    h3 = bf(rn((B, L3)) * t3)
    c3 = bf(rn((B, L3)))
    Wih3_words, Wih3_scales = pack_weight(np.ascontiguousarray((rn((NG * L3, L2)) * 2.0 / np.sqrt(L2) / t2).T), FMT)
    Whh3_words, Whh3_scales = pack_weight(np.ascontiguousarray((rn((NG * L3, L3)) * 0.7 / np.sqrt(L3) / t3).T), FMT)
    bih3 = bf(rn(NG * L3) * 0.3)
    bhh3 = bf(rn(NG * L3) * 0.3)
    Wd_words, Wd_scales = pack_weight(np.ascontiguousarray((rn((L3, S)) * 0.5 / np.sqrt(S) / s).T), FMT)
    bd = bf(rn(L3) * 0.2)
    Wm_words, Wm_scales = pack_weight(np.ascontiguousarray((rn((M, L3)) * 3.0 / np.sqrt(L3)).T), FMT)
    bm = bf(rn(M) * 0.5)
    return {
        "x": x,
        "y2": y2,
        "h3": h3, "c3": c3,
        "Wih3_words": Wih3_words, "Wih3_scales": Wih3_scales,
        "Whh3_words": Whh3_words, "Whh3_scales": Whh3_scales,
        "bih3": bih3, "bhh3": bhh3,
        "Wd_words": Wd_words, "Wd_scales": Wd_scales, "bd": bd,
        "Wm_words": Wm_words, "Wm_scales": Wm_scales, "bm": bm,
    }


def reference(x, y2, h3, c3, Wih3_words, Wih3_scales, Whh3_words, Whh3_scales, bih3, bhh3, Wd_words, Wd_scales, bd, Wm_words, Wm_scales, bm):
    y3, nc3 = lstm_cell(f64(y2), f64(h3), f64(c3), unpack_weight(Wih3_words, Wih3_scales, FMT), unpack_weight(Whh3_words, Whh3_scales, FMT), f64(bih3), f64(bhh3))
    mid = (mxq(f64(x), 1, "e4m3") @ unpack_weight(Wd_words, Wd_scales, FMT)) + f64(bd) + y3
    motors = (mxq(mid, 1, "e4m3") @ unpack_weight(Wm_words, Wm_scales, FMT)) + f64(bm)
    return log_softmax(motors), y3, nc3

@@ -1,0 +1,345 @@
+from contextlib import ExitStack
+
+import concourse.mybir as mybir
+from concourse.masks import make_identity
+
+FP8X4 = mybir.dt.float8_e4m3fn_x4
+BF16 = mybir.dt.bfloat16
+F32 = mybir.dt.float32
+I32 = mybir.dt.int32
+U32 = mybir.dt.uint32
+U8 = mybir.dt.uint8
+ACT = mybir.ActivationFunctionType
+AX = mybir.AxisListType
+
+P = 128
+NB = 2
+GROUP = 512
+BANK = 512
+L3 = 512
+GATES = 4
+Y2_GROUPS = 16
+STAGE = 4
+STAGES = Y2_GROUPS // STAGE
+EARLY_GATES = 3
+O_GATE = 3
+O_GROUPS_PER_LOAD = 2
+LATE_LOADS = Y2_GROUPS // O_GROUPS_PER_LOAD
+LATE_BUFS = 4
+
+FLOPS = 2 * 256 * (8192 * 2048 + 512 * 2048 + 512 * 512 + 512 * 512)
+
+
+def tile_network_pb_k_kernel(
+    tc, x, y2, h3, c3,
+    Wih3_words, Wih3_scales, Whh3_words, Whh3_scales, bih3, bhh3,
+    Wd_words, Wd_scales, bd, Wm_words, Wm_scales, bm,
+    out_0, out_1, out_2,
+):
+    nc = tc.nc
+    with ExitStack() as ctx:
+        ctx.enter_context(tc.manual_schedule())
+        keep = ctx.enter_context(tc.tile_pool(name="keep", bufs=1))
+        y2_pool = ctx.enter_context(tc.tile_pool(name="y2_pool", bufs=STAGES))
+        grouped_pool = ctx.enter_context(tc.tile_pool(name="grouped_pool", bufs=2))
+        early_pool = ctx.enter_context(tc.tile_pool(name="early_pool", bufs=2 * STAGE))
+        late_pool = ctx.enter_context(tc.tile_pool(name="late_pool", bufs=LATE_BUFS))
+        psum = ctx.enter_context(tc.psum_pool(name="psum", bufs=1))
+
+        def bank_tile(n, name):
+            return psum.tile([P, BANK], F32, tag="bank%d" % n, name=name)
+
+        bias_rows = keep.tile([P, 6 * BANK], BF16)
+        nc.vector.memset(bias_rows[:], 0.0)
+        ones = keep.tile([P, P], BF16)
+        nc.vector.memset(ones[:], 1.0)
+        wih_planes = keep.tile([P, STAGES * GATES * L3], U8, align_bytes=64)
+        nc.vector.memset(wih_planes[:].bitcast(I32), 0)
+        small_planes = keep.tile([P, GATES * L3], U8, align_bytes=64)
+        nc.vector.memset(small_planes[:].bitcast(I32), 0)
+        ident_f32 = keep.tile([P, P], F32)
+        make_identity(nc, ident_f32[:])
+        ident_bf16 = keep.tile([P, P], BF16)
+        make_identity(nc, ident_bf16[:])
+
+        nc.scalar.dma_start(out=bias_rows[0:1, 0 : GATES * L3], in_=bih3.unsqueeze(0))
+        nc.scalar.dma_start(out=bias_rows[1:2, 0 : GATES * L3], in_=bhh3.unsqueeze(0))
+        nc.scalar.dma_start(out=bias_rows[0:1, 4 * BANK : 5 * BANK], in_=bd.unsqueeze(0))
+        nc.scalar.dma_start(out=bias_rows[0:1, 5 * BANK : 6 * BANK], in_=bm.unsqueeze(0))
+
+        def load_small_plane(offset, scales, width):
+            for quadrant in range(4):
+                first = 32 * quadrant + offset
+                nc.sync.dma_start(
+                    out=small_planes[first : first + 4, 0:width].bitcast(I32),
+                    in_=scales[0, 4 * quadrant : 4 * quadrant + 4, :].bitcast(I32),
+                )
+
+        y2_rows = y2.rearrange("(b p) k -> p b k", p=P)
+        y2_chunks = []
+        for stage in range(STAGES):
+            y2_chunk = y2_pool.tile([P, NB, STAGE * GROUP], BF16)
+            nc.sync.dma_start(out=y2_chunk[:], in_=y2_rows[:, :, stage * STAGE * GROUP : (stage + 1) * STAGE * GROUP])
+            y2_chunks.append(y2_chunk)
+        h3_sb = keep.tile([P, NB, GROUP], BF16)
+        nc.sync.dma_start(out=h3_sb[:], in_=h3.rearrange("(b p) k -> p b k", p=P))
+        x_sb = keep.tile([P, NB, GROUP], BF16)
+        nc.sync.dma_start(out=x_sb[:], in_=x.rearrange("(b p) k -> p b k", p=P))
+
+        wd_words = keep.tile([P, L3], U32, align_bytes=64)
+        whh_words = keep.tile([P, GATES * L3], U32, align_bytes=64)
+        wm_words = keep.tile([P, L3], U32, align_bytes=64)
+        c3_sb = keep.tile([P, NB, L3], BF16)
+
+        def load_words(tile_words, words):
+            nc.sync.dma_start(out=tile_words[:].bitcast(I32), in_=words[0].rearrange("p n t -> p (n t)").bitcast(I32))
+
+        wih_early = []
+
+        def load_early_stage(stage):
+            for quadrant in range(4):
+                nc.sync.dma_start(
+                    out=wih_planes[32 * quadrant : 32 * quadrant + 16, stage * GATES * L3 : (stage + 1) * GATES * L3].bitcast(I32),
+                    in_=Wih3_scales[stage * STAGE : (stage + 1) * STAGE, 4 * quadrant : 4 * quadrant + 4, :].bitcast(I32),
+                )
+            for g in range(stage * STAGE, (stage + 1) * STAGE):
+                early = early_pool.tile([P, EARLY_GATES * L3], U32, align_bytes=64)
+                nc.sync.dma_start(
+                    out=early[:].bitcast(I32),
+                    in_=Wih3_words[g].rearrange("p n t -> p (n t)")[:, 0 : 4 * EARLY_GATES * L3].bitcast(I32),
+                )
+                wih_early.append(early)
+
+        wih_late = []
+
+        def load_late(n):
+            first = n * O_GROUPS_PER_LOAD
+            late = late_pool.tile([P, O_GROUPS_PER_LOAD, L3], U32, align_bytes=64)
+            nc.sync.dma_start(
+                out=late[:].bitcast(I32),
+                in_=Wih3_words[first : first + O_GROUPS_PER_LOAD]
+                .rearrange("g p n t -> p g (n t)")[:, :, 4 * O_GATE * L3 : 4 * GATES * L3]
+                .bitcast(I32),
+            )
+            wih_late.append(late)
+
+        load_early_stage(0)
+        load_small_plane(4, Wd_scales, L3)
+        load_words(wd_words, Wd_words)
+        load_early_stage(1)
+
+        def transpose_group(words, bank):
+            for b in range(NB):
+                for u in range(2):
+                    piece = (2 * b + u) * P
+                    nc.tensor.transpose(bank[:, piece : piece + P], words[:, b, u : GROUP // 2 : 2], ident_f32[:])
+
+        def bank_as_words(bank):
+            return bank[:].rearrange("p (b u r) -> p b r u", b=NB, u=2)
+
+        def grouped_as_words(grouped, n):
+            return grouped[:].bitcast(F32)[:, n * BANK : (n + 1) * BANK].rearrange("p (b r u) -> p b r u", b=NB, u=2)
+
+        def y2_col(g, b):
+            return (g * NB + b) * P
+
+        y2_codes = keep.tile([P, Y2_GROUPS * NB * P], U32, align_bytes=64)
+        y2_planes = keep.tile([P, Y2_GROUPS * NB * P], U8, align_bytes=64)
+        hx_codes = keep.tile([P, 2 * NB * P], U32, align_bytes=64)
+        hx_planes = keep.tile([P, 2 * NB * P], U8, align_bytes=64)
+
+        def quantise_stage(stage, grouped):
+            cols = slice(y2_col(stage * STAGE, 0), y2_col((stage + 1) * STAGE, 0))
+            nc.vector.quantize_mx(out=y2_codes[:, cols].bitcast(FP8X4), scales=y2_planes[:, cols], in_=grouped[:])
+
+        grouped_before = None
+        for stage in range(STAGES):
+            grouped = grouped_pool.tile([P, STAGE * NB * P * 4], BF16, align_bytes=64)
+            chunk_words = y2_chunks[stage][:].bitcast(F32)
+            for n in range(STAGE):
+                g = stage * STAGE + n
+                turned = bank_tile(g % 8, "turned")
+                transpose_group(chunk_words[:, :, n * (GROUP // 2) : (n + 1) * (GROUP // 2)], turned)
+                if n == 0:
+                    nc.vector.tensor_copy(out=grouped_as_words(grouped, n), in_=bank_as_words(turned))
+                else:
+                    nc.scalar.copy(out=grouped_as_words(grouped, n), in_=bank_as_words(turned))
+            if stage > 0:
+                quantise_stage(stage - 1, grouped_before)
+            grouped_before = grouped
+        grouped_hx = grouped_pool.tile([P, 2 * NB * P * 4], BF16, tag="grouped", align_bytes=64)
+        turned_h3 = bank_tile(0, "turned_h3")
+        transpose_group(h3_sb[:].bitcast(F32), turned_h3)
+        nc.scalar.copy(out=grouped_as_words(grouped_hx, 0), in_=bank_as_words(turned_h3))
+        turned_x = bank_tile(1, "turned_x")
+        transpose_group(x_sb[:].bitcast(F32), turned_x)
+        nc.vector.tensor_copy(out=grouped_as_words(grouped_hx, 1), in_=bank_as_words(turned_x))
+        quantise_stage(STAGES - 1, grouped_before)
+        nc.vector.quantize_mx(out=hx_codes[:].bitcast(FP8X4), scales=hx_planes[:], in_=grouped_hx[:])
+        H3_COL = 0
+        X_COL = NB * P
+
+        def mx_pass(acc, codes, planes, col, weight, weight_plane, start, stop):
+            nc.tensor.matmul_mx(
+                out=acc[:],
+                lhsT=codes[:, col : col + P].bitcast(FP8X4),
+                lhsT_scale=planes[:, col : col + P],
+                rhs=weight.bitcast(FP8X4),
+                rhs_scale=weight_plane,
+                start=start,
+                stop=stop,
+            )
+
+        def wih_plane(g, gate):
+            first = (g // STAGE) * GATES * L3 + gate * L3
+            return wih_planes[4 * (g % STAGE) : P, first : first + L3]
+
+        bias_all = keep.tile([P, 6 * BANK], F32)
+        BD_BLOCK = 4
+        BM_BLOCK = 5
+
+        def spread_bias(first_block):
+            for n in range(2):
+                block = slice((first_block + n) * BANK, (first_block + n + 1) * BANK)
+                spread = bank_tile(n, "spread")
+                nc.tensor.matmul(out=spread[:], lhsT=ones[:], rhs=bias_rows[:, block], start=True, stop=True)
+                nc.scalar.copy(out=bias_all[:, block], in_=spread[:])
+
+        skip = []
+
+        def skip_projection():
+            for b in range(NB):
+                skip_acc = bank_tile(b, "skip_acc")
+                mx_pass(skip_acc, hx_codes, hx_planes, X_COL + b * P, wd_words[:], small_planes[4:P, 0:L3], True, True)
+                skip_b = keep.tile([P, L3], F32, name="skip_b%d" % b)
+                nc.vector.tensor_add(out=skip_b[:], in0=skip_acc[:], in1=bias_all[:, BD_BLOCK * BANK : (BD_BLOCK + 1) * BANK])
+                skip.append(skip_b)
+
+        early_acc = [[bank_tile(2 + EARLY_GATES * b + gate, "early_acc") for gate in range(EARLY_GATES)] for b in range(NB)]
+
+        def early_stage(stage):
+            for g in range(stage * STAGE, (stage + 1) * STAGE):
+                for b in range(NB):
+                    for gate in range(EARLY_GATES):
+                        mx_pass(
+                            early_acc[b][gate], y2_codes, y2_planes, y2_col(g, b),
+                            wih_early[g][:, gate * L3 : (gate + 1) * L3], wih_plane(g, gate), g == 0, False,
+                        )
+
+        warm = keep.tile([P, 2], F32)
+        early_stage(0)
+        load_early_stage(2)
+        spread_bias(BD_BLOCK)
+        early_stage(1)
+        load_early_stage(3)
+        load_small_plane(0, Whh3_scales, GATES * L3)
+        load_words(whh_words, Whh3_words)
+        nc.sync.dma_start(out=c3_sb[:], in_=c3.rearrange("(b p) k -> p b k", p=P))
+        for n in range(LATE_BUFS):
+            load_late(n)
+        skip_projection()
+        early_stage(2)
+        spread_bias(0)
+        early_stage(3)
+        spread_bias(2)
+        nc.scalar.activation(out=warm[:, 0:1], in_=bias_all[:, 0:1], func=ACT.Sigmoid)
+        for b in range(NB):
+            for gate in range(EARLY_GATES):
+                mx_pass(
+                    early_acc[b][gate], hx_codes, hx_planes, H3_COL + b * P,
+                    whh_words[:, gate * L3 : (gate + 1) * L3], small_planes[:, gate * L3 : (gate + 1) * L3], False, True,
+                )
+
+        o_acc = [bank_tile(b, "o_acc") for b in range(NB)]
+        for b in range(NB):
+            mx_pass(
+                o_acc[b], hx_codes, hx_planes, H3_COL + b * P,
+                whh_words[:, O_GATE * L3 : GATES * L3], small_planes[:, O_GATE * L3 : GATES * L3], True, False,
+            )
+        for g in range(Y2_GROUPS):
+            for b in range(NB):
+                mx_pass(
+                    o_acc[b], y2_codes, y2_planes, y2_col(g, b),
+                    wih_late[g // O_GROUPS_PER_LOAD][:, g % O_GROUPS_PER_LOAD, :], wih_plane(g, O_GATE),
+                    False, g == Y2_GROUPS - 1,
+                )
+            if g % O_GROUPS_PER_LOAD == O_GROUPS_PER_LOAD - 1 and len(wih_late) < LATE_LOADS:
+                load_late(len(wih_late))
+        load_small_plane(8, Wm_scales, L3)
+        load_words(wm_words, Wm_words)
+
+        gate_val = [[keep.tile([P, L3], F32, name="gate_val%d%d" % (b, gate)) for gate in range(GATES)] for b in range(NB)]
+
+        def gate_value(b, gate, acc, func):
+            value = gate_val[b][gate]
+            nc.vector.tensor_add(out=value[:], in0=acc[:], in1=bias_all[:, gate * L3 : (gate + 1) * L3])
+            nc.scalar.activation(out=value[:], in_=value[:], func=func)
+
+        for b in range(NB):
+            gate_value(b, 0, early_acc[b][0], ACT.Sigmoid)
+            gate_value(b, 1, early_acc[b][1], ACT.Sigmoid)
+            gate_value(b, 2, early_acc[b][2], ACT.Tanh)
+        tanh_cell = []
+        for b in range(NB):
+            i_val, f_val, g_val = gate_val[b][0], gate_val[b][1], gate_val[b][2]
+            nc.vector.tensor_mul(out=f_val[:], in0=f_val[:], in1=c3_sb[:, b, :])
+            nc.vector.tensor_mul(out=i_val[:], in0=i_val[:], in1=g_val[:])
+            cell = keep.tile([P, L3], F32, name="cell%d" % b)
+            nc.vector.tensor_add(out=cell[:], in0=f_val[:], in1=i_val[:])
+            nc.sync.dma_start(out=out_2[b * P : (b + 1) * P, :], in_=cell[:])
+            tanh_b = keep.tile([P, L3], F32, name="tanh_cell%d" % b)
+            nc.scalar.activation(out=tanh_b[:], in_=cell[:], func=ACT.Tanh)
+            tanh_cell.append(tanh_b)
+
+        for b in range(NB):
+            gate_value(b, O_GATE, o_acc[b], ACT.Sigmoid)
+        nc.scalar.activation(out=warm[:, 1:2], in_=bias_all[:, 0:1], func=ACT.Exp)
+        mid = []
+        for b in range(NB):
+            y3_b = keep.tile([P, L3], F32, name="y3_b%d" % b)
+            nc.vector.tensor_mul(out=y3_b[:], in0=gate_val[b][O_GATE][:], in1=tanh_cell[b][:])
+            nc.sync.dma_start(out=out_1[b * P : (b + 1) * P, :], in_=y3_b[:])
+            mid_b = keep.tile([P, L3], BF16, name="mid_b%d" % b)
+            nc.vector.tensor_add(out=mid_b[:], in0=y3_b[:], in1=skip[b][:])
+            mid.append(mid_b)
+
+        mid_codes = keep.tile([P, NB * P], U32, align_bytes=64)
+        mid_planes = keep.tile([P, NB * P], U8, align_bytes=64)
+        grouped_mid = []
+        for b in range(NB):
+            turned_mid = psum.tile([P, 4, P], BF16, tag="bank%d" % (2 + EARLY_GATES * b), name="turned_mid")
+            for t in range(4):
+                nc.tensor.transpose(turned_mid[:, t, :], mid[b][:, t:L3:4], ident_bf16[:])
+            grouped_b = keep.tile([P, P, 4], BF16, name="grouped_mid%d" % b, align_bytes=64)
+            nc.scalar.copy(out=grouped_b[:], in_=turned_mid[:].rearrange("p t r -> p r t"))
+            grouped_mid.append(grouped_b)
+        for b in range(NB):
+            nc.vector.quantize_mx(
+                out=mid_codes[:, b * P : (b + 1) * P].bitcast(FP8X4),
+                scales=mid_planes[:, b * P : (b + 1) * P],
+                in_=grouped_mid[b][:].rearrange("p r t -> p (r t)"),
+            )
+
+        neg_max = keep.tile([P, NB], F32)
+        exp_sum = keep.tile([P, NB], F32)
+        log_sum = keep.tile([P, NB], F32)
+        shift = keep.tile([P, NB], F32)
+        motors = []
+        for b in range(NB):
+            motors_acc = bank_tile(3 + EARLY_GATES * b, "motors_acc")
+            mx_pass(motors_acc, mid_codes, mid_planes, b * P, wm_words[:], small_planes[8:P, 0:L3], True, True)
+            motors_b = keep.tile([P, L3], F32, name="motors_b%d" % b)
+            nc.vector.tensor_add(out=motors_b[:], in0=motors_acc[:], in1=bias_all[:, BM_BLOCK * BANK : (BM_BLOCK + 1) * BANK])
+            nc.vector.reduce_max(out=neg_max[:, b : b + 1], in_=motors_b[:], axis=AX.X, negate=True)
+            exp_b = keep.tile([P, L3], BF16, name="exp_b%d" % b)
+            nc.scalar.activation(
+                out=exp_b[:], in_=motors_b[:], func=ACT.Exp, bias=neg_max[:, b : b + 1], scale=1.0,
+                accum_out=exp_sum[:, b : b + 1],
+            )
+            motors.append(motors_b)
+        nc.scalar.activation(out=log_sum[:], in_=exp_sum[:], func=ACT.Ln)
+        nc.vector.tensor_sub(out=shift[:], in0=neg_max[:], in1=log_sum[:])
+        nc.vector.tensor_scalar_add(out=motors[0][:], in0=motors[0][:], scalar1=shift[:, 0:1])
+        nc.scalar.activation(out=motors[1][:], in_=motors[1][:], func=ACT.Identity, bias=shift[:, 1:2], scale=1.0)
+        for b in range(NB):
+            nc.sync.dma_start(out=out_0[b * P : (b + 1) * P, :], in_=motors[b][:])

@@ -24,8 +24,6 @@ STAGES = Y2_GROUPS // STAGE
 EARLY_GATES = 3
 O_GATE = 3
 O_GROUPS_PER_LOAD = 2
-LATE_LOADS = Y2_GROUPS // O_GROUPS_PER_LOAD
-LATE_BUFS = 4
 
 FLOPS = 2 * 256 * (8192 * 2048 + 512 * 2048 + 512 * 512 + 512 * 512)
 
@@ -43,7 +41,6 @@ def tile_network_pb_k_kernel(
         y2_pool = ctx.enter_context(tc.tile_pool(name="y2_pool", bufs=STAGES))
         grouped_pool = ctx.enter_context(tc.tile_pool(name="grouped_pool", bufs=2))
         early_pool = ctx.enter_context(tc.tile_pool(name="early_pool", bufs=2 * STAGE))
-        late_pool = ctx.enter_context(tc.tile_pool(name="late_pool", bufs=LATE_BUFS))
         psum = ctx.enter_context(tc.psum_pool(name="psum", bufs=1))
 
         def bank_tile(n, name):
@@ -55,8 +52,12 @@ def tile_network_pb_k_kernel(
         nc.vector.memset(ones[:], 1.0)
         wih_planes = keep.tile([P, STAGES * GATES * L3], U8, align_bytes=64)
         nc.vector.memset(wih_planes[:].bitcast(I32), 0)
-        small_planes = keep.tile([P, GATES * L3], U8, align_bytes=64)
-        nc.vector.memset(small_planes[:].bitcast(I32), 0)
+        whh_plane = keep.tile([P, GATES * L3], U8, align_bytes=64)
+        nc.vector.memset(whh_plane[:].bitcast(I32), 0)
+        wd_plane = keep.tile([P, L3], U8, align_bytes=64)
+        nc.vector.memset(wd_plane[:].bitcast(I32), 0)
+        wm_plane = keep.tile([P, L3], U8, align_bytes=64)
+        nc.vector.memset(wm_plane[:].bitcast(I32), 0)
         ident_f32 = keep.tile([P, P], F32)
         make_identity(nc, ident_f32[:])
         ident_bf16 = keep.tile([P, P], BF16)
@@ -67,18 +68,17 @@ def tile_network_pb_k_kernel(
         nc.scalar.dma_start(out=bias_rows[0:1, 4 * BANK : 5 * BANK], in_=bd.unsqueeze(0))
         nc.scalar.dma_start(out=bias_rows[0:1, 5 * BANK : 6 * BANK], in_=bm.unsqueeze(0))
 
-        def load_small_plane(offset, scales, width):
+        def load_plane(plane, scales):
             for quadrant in range(4):
-                first = 32 * quadrant + offset
                 nc.sync.dma_start(
-                    out=small_planes[first : first + 4, 0:width].bitcast(I32),
+                    out=plane[32 * quadrant : 32 * quadrant + 4, :].bitcast(I32),
                     in_=scales[0, 4 * quadrant : 4 * quadrant + 4, :].bitcast(I32),
                 )
 
         y2_rows = y2.rearrange("(b p) k -> p b k", p=P)
         y2_chunks = []
         for stage in range(STAGES):
-            y2_chunk = y2_pool.tile([P, NB, STAGE * GROUP], BF16)
+            y2_chunk = y2_pool.tile([P, NB, STAGE * GROUP], BF16, tag="chunk", align_bytes=64)
             nc.sync.dma_start(out=y2_chunk[:], in_=y2_rows[:, :, stage * STAGE * GROUP : (stage + 1) * STAGE * GROUP])
             y2_chunks.append(y2_chunk)
         h3_sb = keep.tile([P, NB, GROUP], BF16)
@@ -112,19 +112,20 @@ def tile_network_pb_k_kernel(
 
         wih_late = []
 
-        def load_late(n):
-            first = n * O_GROUPS_PER_LOAD
-            late = late_pool.tile([P, O_GROUPS_PER_LOAD, L3], U32, align_bytes=64)
-            nc.sync.dma_start(
-                out=late[:].bitcast(I32),
-                in_=Wih3_words[first : first + O_GROUPS_PER_LOAD]
-                .rearrange("g p n t -> p g (n t)")[:, :, 4 * O_GATE * L3 : 4 * GATES * L3]
-                .bitcast(I32),
-            )
+        def load_late_stage(stage):
+            late = y2_pool.tile([P, STAGE, L3], U32, tag="chunk", align_bytes=64)
+            for n in range(0, STAGE, O_GROUPS_PER_LOAD):
+                first = stage * STAGE + n
+                nc.sync.dma_start(
+                    out=late[:, n : n + O_GROUPS_PER_LOAD, :].bitcast(I32),
+                    in_=Wih3_words[first : first + O_GROUPS_PER_LOAD]
+                    .rearrange("g p n t -> p g (n t)")[:, :, 4 * O_GATE * L3 : 4 * GATES * L3]
+                    .bitcast(I32),
+                )
             wih_late.append(late)
 
         load_early_stage(0)
-        load_small_plane(4, Wd_scales, L3)
+        load_plane(wd_plane, Wd_scales)
         load_words(wd_words, Wd_words)
         load_early_stage(1)
 
@@ -210,7 +211,7 @@ def tile_network_pb_k_kernel(
         def skip_projection():
             for b in range(NB):
                 skip_acc = bank_tile(b, "skip_acc")
-                mx_pass(skip_acc, hx_codes, hx_planes, X_COL + b * P, wd_words[:], small_planes[4:P, 0:L3], True, True)
+                mx_pass(skip_acc, hx_codes, hx_planes, X_COL + b * P, wd_words[:], wd_plane[:], True, True)
                 skip_b = keep.tile([P, L3], F32, name="skip_b%d" % b)
                 nc.vector.tensor_add(out=skip_b[:], in0=skip_acc[:], in1=bias_all[:, BD_BLOCK * BANK : (BD_BLOCK + 1) * BANK])
                 skip.append(skip_b)
@@ -232,11 +233,13 @@ def tile_network_pb_k_kernel(
         spread_bias(BD_BLOCK)
         early_stage(1)
         load_early_stage(3)
-        load_small_plane(0, Whh3_scales, GATES * L3)
+        load_plane(whh_plane, Whh3_scales)
         load_words(whh_words, Whh3_words)
         nc.sync.dma_start(out=c3_sb[:], in_=c3.rearrange("(b p) k -> p b k", p=P))
-        for n in range(LATE_BUFS):
-            load_late(n)
+        for stage in range(STAGES):
+            load_late_stage(stage)
+        load_plane(wm_plane, Wm_scales)
+        load_words(wm_words, Wm_words)
         skip_projection()
         early_stage(2)
         spread_bias(0)
@@ -247,26 +250,22 @@ def tile_network_pb_k_kernel(
             for gate in range(EARLY_GATES):
                 mx_pass(
                     early_acc[b][gate], hx_codes, hx_planes, H3_COL + b * P,
-                    whh_words[:, gate * L3 : (gate + 1) * L3], small_planes[:, gate * L3 : (gate + 1) * L3], False, True,
+                    whh_words[:, gate * L3 : (gate + 1) * L3], whh_plane[:, gate * L3 : (gate + 1) * L3], False, True,
                 )
 
         o_acc = [bank_tile(b, "o_acc") for b in range(NB)]
         for b in range(NB):
             mx_pass(
                 o_acc[b], hx_codes, hx_planes, H3_COL + b * P,
-                whh_words[:, O_GATE * L3 : GATES * L3], small_planes[:, O_GATE * L3 : GATES * L3], True, False,
+                whh_words[:, O_GATE * L3 : GATES * L3], whh_plane[:, O_GATE * L3 : GATES * L3], True, False,
             )
         for g in range(Y2_GROUPS):
             for b in range(NB):
                 mx_pass(
                     o_acc[b], y2_codes, y2_planes, y2_col(g, b),
-                    wih_late[g // O_GROUPS_PER_LOAD][:, g % O_GROUPS_PER_LOAD, :], wih_plane(g, O_GATE),
+                    wih_late[g // STAGE][:, g % STAGE, :], wih_plane(g, O_GATE),
                     False, g == Y2_GROUPS - 1,
                 )
-            if g % O_GROUPS_PER_LOAD == O_GROUPS_PER_LOAD - 1 and len(wih_late) < LATE_LOADS:
-                load_late(len(wih_late))
-        load_small_plane(8, Wm_scales, L3)
-        load_words(wm_words, Wm_words)
 
         gate_val = [[keep.tile([P, L3], F32, name="gate_val%d%d" % (b, gate)) for gate in range(GATES)] for b in range(NB)]
 
@@ -327,7 +326,7 @@ def tile_network_pb_k_kernel(
         motors = []
         for b in range(NB):
             motors_acc = bank_tile(3 + EARLY_GATES * b, "motors_acc")
-            mx_pass(motors_acc, mid_codes, mid_planes, b * P, wm_words[:], small_planes[8:P, 0:L3], True, True)
+            mx_pass(motors_acc, mid_codes, mid_planes, b * P, wm_words[:], wm_plane[:], True, True)
             motors_b = keep.tile([P, L3], F32, name="motors_b%d" % b)
             nc.vector.tensor_add(out=motors_b[:], in0=motors_acc[:], in1=bias_all[:, BM_BLOCK * BANK : (BM_BLOCK + 1) * BANK])
             nc.vector.reduce_max(out=neg_max[:, b : b + 1], in_=motors_b[:], axis=AX.X, negate=True)

@@ -96,12 +96,14 @@ def tile_network_pb_k_kernel(
 
         wih_early = []
 
-        def load_early_stage(stage):
+        def load_wih_planes(stage):
             for quadrant in range(4):
                 nc.sync.dma_start(
                     out=wih_planes[32 * quadrant : 32 * quadrant + 16, stage * GATES * L3 : (stage + 1) * GATES * L3].bitcast(I32),
                     in_=Wih3_scales[stage * STAGE : (stage + 1) * STAGE, 4 * quadrant : 4 * quadrant + 4, :].bitcast(I32),
                 )
+
+        def load_early_stage(stage):
             for g in range(stage * STAGE, (stage + 1) * STAGE):
                 early = early_pool.tile([P, EARLY_GATES * L3], U32, align_bytes=64)
                 nc.sync.dma_start(
@@ -124,8 +126,11 @@ def tile_network_pb_k_kernel(
                 )
             wih_late.append(late)
 
-        load_early_stage(0)
+        for stage in range(STAGES):
+            load_wih_planes(stage)
         load_plane(wd_plane, Wd_scales)
+        load_plane(whh_plane, Whh3_scales)
+        load_early_stage(0)
         load_words(wd_words, Wd_words)
         load_early_stage(1)
 
@@ -233,7 +238,6 @@ def tile_network_pb_k_kernel(
         spread_bias(BD_BLOCK)
         early_stage(1)
         load_early_stage(3)
-        load_plane(whh_plane, Whh3_scales)
         load_words(whh_words, Whh3_words)
         nc.sync.dma_start(out=c3_sb[:], in_=c3.rearrange("(b p) k -> p b k", p=P))
         for stage in range(STAGES):

@@ -70,10 +70,25 @@ def tile_network_pb_k_kernel(
 
         def load_plane(plane, scales):
             for quadrant in range(4):
-                nc.sync.dma_start(
-                    out=plane[32 * quadrant : 32 * quadrant + 4, :].bitcast(I32),
-                    in_=scales[0, 4 * quadrant : 4 * quadrant + 4, :].bitcast(I32),
+                nc.gpsimd.dma_start(
+                    out=plane[32 * quadrant : 32 * quadrant + 4, :].bitcast(F32),
+                    in_=scales[0, 4 * quadrant : 4 * quadrant + 4, :].bitcast(F32),
                 )
+
+        def load_wih_planes(stage):
+            for quadrant in range(4):
+                nc.gpsimd.dma_start(
+                    out=wih_planes[32 * quadrant : 32 * quadrant + 16, stage * GATES * L3 : (stage + 1) * GATES * L3].bitcast(F32),
+                    in_=Wih3_scales[stage * STAGE : (stage + 1) * STAGE, 4 * quadrant : 4 * quadrant + 4, :].bitcast(F32),
+                )
+
+        load_wih_planes(0)
+        load_wih_planes(1)
+        load_plane(wd_plane, Wd_scales)
+        load_wih_planes(2)
+        load_wih_planes(3)
+        load_plane(whh_plane, Whh3_scales)
+        load_plane(wm_plane, Wm_scales)
 
         y2_rows = y2.rearrange("(b p) k -> p b k", p=P)
         y2_chunks = []
@@ -95,13 +110,6 @@ def tile_network_pb_k_kernel(
             nc.sync.dma_start(out=tile_words[:].bitcast(I32), in_=words[0].rearrange("p n t -> p (n t)").bitcast(I32))
 
         wih_early = []
-
-        def load_wih_planes(stage):
-            for quadrant in range(4):
-                nc.sync.dma_start(
-                    out=wih_planes[32 * quadrant : 32 * quadrant + 16, stage * GATES * L3 : (stage + 1) * GATES * L3].bitcast(I32),
-                    in_=Wih3_scales[stage * STAGE : (stage + 1) * STAGE, 4 * quadrant : 4 * quadrant + 4, :].bitcast(I32),
-                )
 
         def load_early_stage(stage):
             for g in range(stage * STAGE, (stage + 1) * STAGE):
@@ -126,10 +134,6 @@ def tile_network_pb_k_kernel(
                 )
             wih_late.append(late)
 
-        for stage in range(STAGES):
-            load_wih_planes(stage)
-        load_plane(wd_plane, Wd_scales)
-        load_plane(whh_plane, Whh3_scales)
         load_early_stage(0)
         load_words(wd_words, Wd_words)
         load_early_stage(1)
@@ -242,7 +246,6 @@ def tile_network_pb_k_kernel(
         nc.sync.dma_start(out=c3_sb[:], in_=c3.rearrange("(b p) k -> p b k", p=P))
         for stage in range(STAGES):
             load_late_stage(stage)
-        load_plane(wm_plane, Wm_scales)
         load_words(wm_words, Wm_words)
         skip_projection()
         early_stage(2)

from contextlib import ExitStack

import concourse.mybir as mybir
from concourse.masks import make_identity

FP8X4 = mybir.dt.float8_e4m3fn_x4
BF16 = mybir.dt.bfloat16
F32 = mybir.dt.float32
I32 = mybir.dt.int32
U32 = mybir.dt.uint32
U8 = mybir.dt.uint8
ACT = mybir.ActivationFunctionType
AX = mybir.AxisListType

P = 128
NB = 2
GROUP = 512
BANK = 512
L3 = 512
GATES = 4
Y2_GROUPS = 16
STAGE = 4
STAGES = Y2_GROUPS // STAGE
EARLY_GATES = 3
O_GATE = 3
O_GROUPS_PER_LOAD = 2

FLOPS = 2 * 256 * (8192 * 2048 + 512 * 2048 + 512 * 512 + 512 * 512)


def tile_network_pb_k_kernel(
    tc, x, y2, h3, c3,
    Wih3_words, Wih3_scales, Whh3_words, Whh3_scales, bih3, bhh3,
    Wd_words, Wd_scales, bd, Wm_words, Wm_scales, bm,
    out_0, out_1, out_2,
):
    nc = tc.nc
    with ExitStack() as ctx:
        ctx.enter_context(tc.manual_schedule())
        keep = ctx.enter_context(tc.tile_pool(name="keep", bufs=1))
        y2_pool = ctx.enter_context(tc.tile_pool(name="y2_pool", bufs=STAGES))
        grouped_pool = ctx.enter_context(tc.tile_pool(name="grouped_pool", bufs=2))
        early_pool = ctx.enter_context(tc.tile_pool(name="early_pool", bufs=2 * STAGE))
        psum = ctx.enter_context(tc.psum_pool(name="psum", bufs=1))

        def bank_tile(n, name):
            return psum.tile([P, BANK], F32, tag="bank%d" % n, name=name)

        bias_rows = keep.tile([P, 6 * BANK], BF16)
        nc.vector.memset(bias_rows[:], 0.0)
        ones = keep.tile([P, P], BF16)
        nc.vector.memset(ones[:], 1.0)
        wih_planes = keep.tile([P, STAGES * GATES * L3], U8, align_bytes=64)
        nc.vector.memset(wih_planes[:].bitcast(I32), 0)
        whh_plane = keep.tile([P, GATES * L3], U8, align_bytes=64)
        nc.vector.memset(whh_plane[:].bitcast(I32), 0)
        wd_plane = keep.tile([P, L3], U8, align_bytes=64)
        nc.vector.memset(wd_plane[:].bitcast(I32), 0)
        wm_plane = keep.tile([P, L3], U8, align_bytes=64)
        nc.vector.memset(wm_plane[:].bitcast(I32), 0)
        ident_f32 = keep.tile([P, P], F32)
        make_identity(nc, ident_f32[:])
        ident_bf16 = keep.tile([P, P], BF16)
        make_identity(nc, ident_bf16[:])

        nc.scalar.dma_start(out=bias_rows[0:1, 0 : GATES * L3], in_=bih3.unsqueeze(0))
        nc.scalar.dma_start(out=bias_rows[1:2, 0 : GATES * L3], in_=bhh3.unsqueeze(0))
        nc.scalar.dma_start(out=bias_rows[0:1, 4 * BANK : 5 * BANK], in_=bd.unsqueeze(0))
        nc.scalar.dma_start(out=bias_rows[0:1, 5 * BANK : 6 * BANK], in_=bm.unsqueeze(0))

        def load_plane(plane, scales):
            for quadrant in range(4):
                nc.gpsimd.dma_start(
                    out=plane[32 * quadrant : 32 * quadrant + 4, :].bitcast(F32),
                    in_=scales[0, 4 * quadrant : 4 * quadrant + 4, :].bitcast(F32),
                )

        def load_wih_planes(stage):
            for quadrant in range(4):
                nc.gpsimd.dma_start(
                    out=wih_planes[32 * quadrant : 32 * quadrant + 16, stage * GATES * L3 : (stage + 1) * GATES * L3].bitcast(F32),
                    in_=Wih3_scales[stage * STAGE : (stage + 1) * STAGE, 4 * quadrant : 4 * quadrant + 4, :].bitcast(F32),
                )

        load_wih_planes(0)
        load_wih_planes(1)
        load_plane(wd_plane, Wd_scales)
        load_wih_planes(2)
        load_wih_planes(3)
        load_plane(whh_plane, Whh3_scales)
        load_plane(wm_plane, Wm_scales)

        y2_rows = y2.rearrange("(b p) k -> p b k", p=P)
        y2_chunks = []
        for stage in range(STAGES):
            y2_chunk = y2_pool.tile([P, NB, STAGE * GROUP], BF16, tag="chunk", align_bytes=64)
            nc.sync.dma_start(out=y2_chunk[:], in_=y2_rows[:, :, stage * STAGE * GROUP : (stage + 1) * STAGE * GROUP])
            y2_chunks.append(y2_chunk)
        h3_sb = keep.tile([P, NB, GROUP], BF16)
        nc.sync.dma_start(out=h3_sb[:], in_=h3.rearrange("(b p) k -> p b k", p=P))
        x_sb = keep.tile([P, NB, GROUP], BF16)
        nc.sync.dma_start(out=x_sb[:], in_=x.rearrange("(b p) k -> p b k", p=P))

        wd_words = keep.tile([P, L3], U32, align_bytes=64)
        whh_words = keep.tile([P, GATES * L3], U32, align_bytes=64)
        wm_words = keep.tile([P, L3], U32, align_bytes=64)
        c3_sb = keep.tile([P, NB, L3], BF16)

        def load_words(tile_words, words):
            nc.sync.dma_start(out=tile_words[:].bitcast(I32), in_=words[0].rearrange("p n t -> p (n t)").bitcast(I32))

        wih_early = []

        def load_early_stage(stage):
            for g in range(stage * STAGE, (stage + 1) * STAGE):
                early = early_pool.tile([P, EARLY_GATES * L3], U32, align_bytes=64)
                nc.sync.dma_start(
                    out=early[:].bitcast(I32),
                    in_=Wih3_words[g].rearrange("p n t -> p (n t)")[:, 0 : 4 * EARLY_GATES * L3].bitcast(I32),
                )
                wih_early.append(early)

        wih_late = []

        def load_late_stage(stage):
            late = y2_pool.tile([P, STAGE, L3], U32, tag="chunk", align_bytes=64)
            for n in range(0, STAGE, O_GROUPS_PER_LOAD):
                first = stage * STAGE + n
                nc.sync.dma_start(
                    out=late[:, n : n + O_GROUPS_PER_LOAD, :].bitcast(I32),
                    in_=Wih3_words[first : first + O_GROUPS_PER_LOAD]
                    .rearrange("g p n t -> p g (n t)")[:, :, 4 * O_GATE * L3 : 4 * GATES * L3]
                    .bitcast(I32),
                )
            wih_late.append(late)

        load_early_stage(0)
        load_words(wd_words, Wd_words)
        load_early_stage(1)

        def transpose_group(words, bank):
            for b in range(NB):
                for u in range(2):
                    piece = (2 * b + u) * P
                    nc.tensor.transpose(bank[:, piece : piece + P], words[:, b, u : GROUP // 2 : 2], ident_f32[:])

        def bank_as_words(bank):
            return bank[:].rearrange("p (b u r) -> p b r u", b=NB, u=2)

        def grouped_as_words(grouped, n):
            return grouped[:].bitcast(F32)[:, n * BANK : (n + 1) * BANK].rearrange("p (b r u) -> p b r u", b=NB, u=2)

        def y2_col(g, b):
            return (g * NB + b) * P

        y2_codes = keep.tile([P, Y2_GROUPS * NB * P], U32, align_bytes=64)
        y2_planes = keep.tile([P, Y2_GROUPS * NB * P], U8, align_bytes=64)
        hx_codes = keep.tile([P, 2 * NB * P], U32, align_bytes=64)
        hx_planes = keep.tile([P, 2 * NB * P], U8, align_bytes=64)

        def quantise_stage(stage, grouped):
            cols = slice(y2_col(stage * STAGE, 0), y2_col((stage + 1) * STAGE, 0))
            nc.vector.quantize_mx(out=y2_codes[:, cols].bitcast(FP8X4), scales=y2_planes[:, cols], in_=grouped[:])

        grouped_before = None
        for stage in range(STAGES):
            grouped = grouped_pool.tile([P, STAGE * NB * P * 4], BF16, align_bytes=64)
            chunk_words = y2_chunks[stage][:].bitcast(F32)
            for n in range(STAGE):
                g = stage * STAGE + n
                turned = bank_tile(g % 8, "turned")
                transpose_group(chunk_words[:, :, n * (GROUP // 2) : (n + 1) * (GROUP // 2)], turned)
                if n == 0:
                    nc.vector.tensor_copy(out=grouped_as_words(grouped, n), in_=bank_as_words(turned))
                else:
                    nc.scalar.copy(out=grouped_as_words(grouped, n), in_=bank_as_words(turned))
            if stage > 0:
                quantise_stage(stage - 1, grouped_before)
            grouped_before = grouped
        grouped_hx = grouped_pool.tile([P, 2 * NB * P * 4], BF16, tag="grouped", align_bytes=64)
        turned_h3 = bank_tile(0, "turned_h3")
        transpose_group(h3_sb[:].bitcast(F32), turned_h3)
        nc.scalar.copy(out=grouped_as_words(grouped_hx, 0), in_=bank_as_words(turned_h3))
        turned_x = bank_tile(1, "turned_x")
        transpose_group(x_sb[:].bitcast(F32), turned_x)
        nc.vector.tensor_copy(out=grouped_as_words(grouped_hx, 1), in_=bank_as_words(turned_x))
        quantise_stage(STAGES - 1, grouped_before)
        nc.vector.quantize_mx(out=hx_codes[:].bitcast(FP8X4), scales=hx_planes[:], in_=grouped_hx[:])
        H3_COL = 0
        X_COL = NB * P

        def mx_pass(acc, codes, planes, col, weight, weight_plane, start, stop):
            nc.tensor.matmul_mx(
                out=acc[:],
                lhsT=codes[:, col : col + P].bitcast(FP8X4),
                lhsT_scale=planes[:, col : col + P],
                rhs=weight.bitcast(FP8X4),
                rhs_scale=weight_plane,
                start=start,
                stop=stop,
            )

        def wih_plane(g, gate):
            first = (g // STAGE) * GATES * L3 + gate * L3
            return wih_planes[4 * (g % STAGE) : P, first : first + L3]

        bias_all = keep.tile([P, 6 * BANK], F32)
        BD_BLOCK = 4
        BM_BLOCK = 5

        def spread_bias(first_block):
            for n in range(2):
                block = slice((first_block + n) * BANK, (first_block + n + 1) * BANK)
                spread = bank_tile(n, "spread")
                nc.tensor.matmul(out=spread[:], lhsT=ones[:], rhs=bias_rows[:, block], start=True, stop=True)
                nc.scalar.copy(out=bias_all[:, block], in_=spread[:])

        skip = []

        def skip_projection():
            for b in range(NB):
                skip_acc = bank_tile(b, "skip_acc")
                mx_pass(skip_acc, hx_codes, hx_planes, X_COL + b * P, wd_words[:], wd_plane[:], True, True)
                skip_b = keep.tile([P, L3], F32, name="skip_b%d" % b)
                nc.vector.tensor_add(out=skip_b[:], in0=skip_acc[:], in1=bias_all[:, BD_BLOCK * BANK : (BD_BLOCK + 1) * BANK])
                skip.append(skip_b)

        early_acc = [[bank_tile(2 + EARLY_GATES * b + gate, "early_acc") for gate in range(EARLY_GATES)] for b in range(NB)]

        def early_stage(stage):
            for g in range(stage * STAGE, (stage + 1) * STAGE):
                for b in range(NB):
                    for gate in range(EARLY_GATES):
                        mx_pass(
                            early_acc[b][gate], y2_codes, y2_planes, y2_col(g, b),
                            wih_early[g][:, gate * L3 : (gate + 1) * L3], wih_plane(g, gate), g == 0, False,
                        )

        warm = keep.tile([P, 2], F32)
        early_stage(0)
        load_early_stage(2)
        spread_bias(BD_BLOCK)
        early_stage(1)
        load_early_stage(3)
        load_words(whh_words, Whh3_words)
        nc.sync.dma_start(out=c3_sb[:], in_=c3.rearrange("(b p) k -> p b k", p=P))
        for stage in range(STAGES):
            load_late_stage(stage)
        load_words(wm_words, Wm_words)
        skip_projection()
        early_stage(2)
        spread_bias(0)
        early_stage(3)
        spread_bias(2)
        nc.scalar.activation(out=warm[:, 0:1], in_=bias_all[:, 0:1], func=ACT.Sigmoid)
        for b in range(NB):
            for gate in range(EARLY_GATES):
                mx_pass(
                    early_acc[b][gate], hx_codes, hx_planes, H3_COL + b * P,
                    whh_words[:, gate * L3 : (gate + 1) * L3], whh_plane[:, gate * L3 : (gate + 1) * L3], False, True,
                )

        o_acc = [bank_tile(b, "o_acc") for b in range(NB)]
        for b in range(NB):
            mx_pass(
                o_acc[b], hx_codes, hx_planes, H3_COL + b * P,
                whh_words[:, O_GATE * L3 : GATES * L3], whh_plane[:, O_GATE * L3 : GATES * L3], True, False,
            )
        for g in range(Y2_GROUPS):
            for b in range(NB):
                mx_pass(
                    o_acc[b], y2_codes, y2_planes, y2_col(g, b),
                    wih_late[g // STAGE][:, g % STAGE, :], wih_plane(g, O_GATE),
                    False, g == Y2_GROUPS - 1,
                )

        gate_val = [[keep.tile([P, L3], F32, name="gate_val%d%d" % (b, gate)) for gate in range(GATES)] for b in range(NB)]

        def gate_value(b, gate, acc, func):
            value = gate_val[b][gate]
            nc.vector.tensor_add(out=value[:], in0=acc[:], in1=bias_all[:, gate * L3 : (gate + 1) * L3])
            nc.scalar.activation(out=value[:], in_=value[:], func=func)

        for b in range(NB):
            gate_value(b, 0, early_acc[b][0], ACT.Sigmoid)
            gate_value(b, 1, early_acc[b][1], ACT.Sigmoid)
            gate_value(b, 2, early_acc[b][2], ACT.Tanh)
        tanh_cell = []
        for b in range(NB):
            i_val, f_val, g_val = gate_val[b][0], gate_val[b][1], gate_val[b][2]
            nc.vector.tensor_mul(out=f_val[:], in0=f_val[:], in1=c3_sb[:, b, :])
            nc.vector.tensor_mul(out=i_val[:], in0=i_val[:], in1=g_val[:])
            cell = keep.tile([P, L3], F32, name="cell%d" % b)
            nc.vector.tensor_add(out=cell[:], in0=f_val[:], in1=i_val[:])
            nc.sync.dma_start(out=out_2[b * P : (b + 1) * P, :], in_=cell[:])
            tanh_b = keep.tile([P, L3], F32, name="tanh_cell%d" % b)
            nc.scalar.activation(out=tanh_b[:], in_=cell[:], func=ACT.Tanh)
            tanh_cell.append(tanh_b)

        for b in range(NB):
            gate_value(b, O_GATE, o_acc[b], ACT.Sigmoid)
        nc.scalar.activation(out=warm[:, 1:2], in_=bias_all[:, 0:1], func=ACT.Exp)
        mid = []
        for b in range(NB):
            y3_b = keep.tile([P, L3], F32, name="y3_b%d" % b)
            nc.vector.tensor_mul(out=y3_b[:], in0=gate_val[b][O_GATE][:], in1=tanh_cell[b][:])
            nc.sync.dma_start(out=out_1[b * P : (b + 1) * P, :], in_=y3_b[:])
            mid_b = keep.tile([P, L3], BF16, name="mid_b%d" % b)
            nc.vector.tensor_add(out=mid_b[:], in0=y3_b[:], in1=skip[b][:])
            mid.append(mid_b)

        mid_codes = keep.tile([P, NB * P], U32, align_bytes=64)
        mid_planes = keep.tile([P, NB * P], U8, align_bytes=64)
        grouped_mid = []
        for b in range(NB):
            turned_mid = psum.tile([P, 4, P], BF16, tag="bank%d" % (2 + EARLY_GATES * b), name="turned_mid")
            for t in range(4):
                nc.tensor.transpose(turned_mid[:, t, :], mid[b][:, t:L3:4], ident_bf16[:])
            grouped_b = keep.tile([P, P, 4], BF16, name="grouped_mid%d" % b, align_bytes=64)
            nc.scalar.copy(out=grouped_b[:], in_=turned_mid[:].rearrange("p t r -> p r t"))
            grouped_mid.append(grouped_b)
        for b in range(NB):
            nc.vector.quantize_mx(
                out=mid_codes[:, b * P : (b + 1) * P].bitcast(FP8X4),
                scales=mid_planes[:, b * P : (b + 1) * P],
                in_=grouped_mid[b][:].rearrange("p r t -> p (r t)"),
            )

        neg_max = keep.tile([P, NB], F32)
        exp_sum = keep.tile([P, NB], F32)
        log_sum = keep.tile([P, NB], F32)
        shift = keep.tile([P, NB], F32)
        motors = []
        for b in range(NB):
            motors_acc = bank_tile(3 + EARLY_GATES * b, "motors_acc")
            mx_pass(motors_acc, mid_codes, mid_planes, b * P, wm_words[:], wm_plane[:], True, True)
            motors_b = keep.tile([P, L3], F32, name="motors_b%d" % b)
            nc.vector.tensor_add(out=motors_b[:], in0=motors_acc[:], in1=bias_all[:, BM_BLOCK * BANK : (BM_BLOCK + 1) * BANK])
            nc.vector.reduce_max(out=neg_max[:, b : b + 1], in_=motors_b[:], axis=AX.X, negate=True)
            exp_b = keep.tile([P, L3], BF16, name="exp_b%d" % b)
            nc.scalar.activation(
                out=exp_b[:], in_=motors_b[:], func=ACT.Exp, bias=neg_max[:, b : b + 1], scale=1.0,
                accum_out=exp_sum[:, b : b + 1],
            )
            motors.append(motors_b)
        nc.scalar.activation(out=log_sum[:], in_=exp_sum[:], func=ACT.Ln)
        nc.vector.tensor_sub(out=shift[:], in0=neg_max[:], in1=log_sum[:])
        nc.vector.tensor_scalar_add(out=motors[0][:], in0=motors[0][:], scalar1=shift[:, 0:1])
        nc.scalar.activation(out=motors[1][:], in_=motors[1][:], func=ACT.Identity, bias=shift[:, 1:2], scale=1.0)
        for b in range(NB):
            nc.sync.dma_start(out=out_0[b * P : (b + 1) * P, :], in_=motors[b][:])
